import numpy as np
import ml_dtypes

BF16 = ml_dtypes.bfloat16


def bf(x):
    return np.asarray(x, np.float32).astype(BF16)


def f32(x):
    return np.asarray(x, np.float32)


def f64(x):
    return np.asarray(x).astype(np.float64)


def striped(idx):
    return np.tile(idx.reshape(-1, 16).T, (8, 1))


C, S, N = 256, 256, 512
NULL = 0
PE_BASE = 10000.0


def pos_encoding(length, dim):
    pos = np.arange(length, dtype=np.float64)[None, :]
    ch = np.arange(dim)[:, None]
    even = (ch - ch % 2).astype(np.float64)
    ang = pos * np.power(PE_BASE, -even / dim)
    return np.where(ch % 2 == 0, np.sin(ang), np.cos(ang))


def setup_inputs():
    emb = np.random.standard_normal((C, S))
    emb[:, NULL] = 0.0
    return {"emb": f32(emb), "pe": f32(pos_encoding(N, C)), "w_vocab": bf(np.random.standard_normal((C, S)) / np.sqrt(C)), "b_vocab": f32(0.1 * np.random.standard_normal((S, 1))), "offs": striped(np.random.permutation(np.tile(np.arange(S), 2))[:N])}


def reference(emb, pe, w_vocab, b_vocab, offs):
    idx = offs[:16].T.reshape(-1)
    x = f64(emb)[:, idx] + f64(pe)
    return f64(w_vocab).T @ x + f64(b_vocab)

@@ -1,0 +1,84 @@
+import concourse.mybir as mybir
+
+F32 = mybir.dt.float32
+BF16 = mybir.dt.bfloat16
+U16 = mybir.dt.uint16
+ADD = mybir.AluOpType.add
+COPY = mybir.ActivationFunctionType.Copy
+IDENTITY = mybir.ActivationFunctionType.Identity
+
+P = 128
+FEATURES = 256
+WORDS = 256
+PLACES = 512
+PIECE = 256
+FEATURE_BLOCKS = FEATURES // P
+WORD_BLOCKS = WORDS // P
+PIECES = PLACES // PIECE
+OFFSET_COLUMNS = PIECE // 16
+
+FLOPS = 2 * FEATURES * WORDS * PLACES
+
+
+def tile_captioningtransformer_kernel(tc, emb, pe, w_vocab, b_vocab, offs, out):
+    nc = tc.nc
+    with (
+        tc.tile_pool(name="held", bufs=1) as held,
+        tc.psum_pool(name="banks", bufs=1) as banks,
+    ):
+        offsets = held.tile([P, PLACES // 16], U16, name="offsets")
+        nc.sync.dma_start(offsets[:], offs)
+        table = [held.tile([P, WORDS], F32, name=f"table{c}") for c in range(FEATURE_BLOCKS)]
+        for c in range(FEATURE_BLOCKS):
+            nc.sync.dma_start(table[c][:], emb[c * P : (c + 1) * P, :])
+        encoding = [
+            [held.tile([P, PIECE], F32, name=f"encoding{c}_{h}") for h in range(PIECES)]
+            for c in range(FEATURE_BLOCKS)
+        ]
+        for h in range(PIECES):
+            for c in range(FEATURE_BLOCKS):
+                nc.scalar.dma_start(
+                    encoding[c][h][:], pe[c * P : (c + 1) * P, h * PIECE : (h + 1) * PIECE]
+                )
+        weights = [held.tile([P, WORDS], BF16, name=f"weights{c}") for c in range(FEATURE_BLOCKS)]
+        for c in range(FEATURE_BLOCKS):
+            nc.gpsimd.dma_start(weights[c][:], w_vocab[c * P : (c + 1) * P, :])
+        bias = [held.tile([P, 1], F32, name=f"bias{v}") for v in range(WORD_BLOCKS)]
+        for v in range(WORD_BLOCKS):
+            nc.gpsimd.dma_start(bias[v][:], b_vocab[v * P : (v + 1) * P, :])
+
+        def embed(h):
+            rounded = []
+            for c in range(FEATURE_BLOCKS):
+                summed = held.tile([P, PIECE], F32, name=f"summed{c}_{h}")
+                picked = table[c][:].indirect(
+                    offsets[:, h * OFFSET_COLUMNS : (h + 1) * OFFSET_COLUMNS]
+                )
+                nc.vector.tensor_tensor(summed[:], picked, encoding[c][h][:], ADD)
+                moving = held.tile([P, PIECE], BF16, name=f"moving{c}_{h}")
+                nc.scalar.activation(moving[:], summed[:], COPY)
+                rounded.append(moving)
+            return rounded
+
+        def project(h, rounded):
+            scores = [
+                banks.tile([P, PIECE], F32, name=f"scores{v}_{h}") for v in range(WORD_BLOCKS)
+            ]
+            for c in range(FEATURE_BLOCKS):
+                for v in range(WORD_BLOCKS):
+                    nc.tensor.matmul(
+                        scores[v][:],
+                        weights[c][:, v * P : (v + 1) * P],
+                        rounded[c][:],
+                        start=(c == 0),
+                        stop=(c == FEATURE_BLOCKS - 1),
+                    )
+            for v in range(WORD_BLOCKS):
+                staged = held.tile([P, PIECE], F32, name=f"staged{v}_{h}")
+                nc.scalar.activation(staged[:], scores[v][:], IDENTITY, bias=bias[v][:])
+                nc.sync.dma_start(
+                    out[v * P : (v + 1) * P, h * PIECE : (h + 1) * PIECE], staged[:]
+                )
+
+        for h in range(PIECES):
+            project(h, embed(h))

@@ -42,10 +42,10 @@ def tile_captioningtransformer_kernel(tc, emb, pe, w_vocab, b_vocab, offs, out):
                 )
         weights = [held.tile([P, WORDS], BF16, name=f"weights{c}") for c in range(FEATURE_BLOCKS)]
         for c in range(FEATURE_BLOCKS):
-            nc.gpsimd.dma_start(weights[c][:], w_vocab[c * P : (c + 1) * P, :])
+            nc.sync.dma_start(weights[c][:], w_vocab[c * P : (c + 1) * P, :])
         bias = [held.tile([P, 1], F32, name=f"bias{v}") for v in range(WORD_BLOCKS)]
         for v in range(WORD_BLOCKS):
-            nc.gpsimd.dma_start(bias[v][:], b_vocab[v * P : (v + 1) * P, :])
+            nc.scalar.dma_start(bias[v][:], b_vocab[v * P : (v + 1) * P, :])
 
         def embed(h):
             rounded = []

@@ -42,10 +42,10 @@ def tile_captioningtransformer_kernel(tc, emb, pe, w_vocab, b_vocab, offs, out):
                 )
         weights = [held.tile([P, WORDS], BF16, name=f"weights{c}") for c in range(FEATURE_BLOCKS)]
         for c in range(FEATURE_BLOCKS):
-            nc.sync.dma_start(weights[c][:], w_vocab[c * P : (c + 1) * P, :])
+            nc.gpsimd.dma_start(weights[c][:], w_vocab[c * P : (c + 1) * P, :])
         bias = [held.tile([P, 1], F32, name=f"bias{v}") for v in range(WORD_BLOCKS)]
         for v in range(WORD_BLOCKS):
-            nc.scalar.dma_start(bias[v][:], b_vocab[v * P : (v + 1) * P, :])
+            nc.sync.dma_start(bias[v][:], b_vocab[v * P : (v + 1) * P, :])
 
         def embed(h):
             rounded = []
@@ -75,10 +75,14 @@ def tile_captioningtransformer_kernel(tc, emb, pe, w_vocab, b_vocab, offs, out):
                     )
             for v in range(WORD_BLOCKS):
                 staged = held.tile([P, PIECE], F32, name=f"staged{v}_{h}")
-                nc.scalar.activation(staged[:], scores[v][:], IDENTITY, bias=bias[v][:])
+                if v % 2 == 0:
+                    nc.scalar.activation(staged[:], scores[v][:], IDENTITY, bias=bias[v][:])
+                else:
+                    nc.vector.tensor_scalar_add(staged[:], scores[v][:], bias[v][:])
                 nc.sync.dma_start(
                     out[v * P : (v + 1) * P, h * PIECE : (h + 1) * PIECE], staged[:]
                 )
 
+        rounded = [embed(h) for h in range(PIECES)]
         for h in range(PIECES):
-            project(h, embed(h))
+            project(h, rounded[h])

@@ -11,11 +11,12 @@ P = 128
 FEATURES = 256
 WORDS = 256
 PLACES = 512
-PIECE = 256
 FEATURE_BLOCKS = FEATURES // P
 WORD_BLOCKS = WORDS // P
-PIECES = PLACES // PIECE
-OFFSET_COLUMNS = PIECE // 16
+HALF = PLACES // 2
+WIDTHS = (256, 256)
+assert sum(WIDTHS) == PLACES
+STARTS = [sum(WIDTHS[:h]) for h in range(len(WIDTHS))]
 
 FLOPS = 2 * FEATURES * WORDS * PLACES
 
@@ -32,13 +33,13 @@ def tile_captioningtransformer_kernel(tc, emb, pe, w_vocab, b_vocab, offs, out):
         for c in range(FEATURE_BLOCKS):
             nc.sync.dma_start(table[c][:], emb[c * P : (c + 1) * P, :])
         encoding = [
-            [held.tile([P, PIECE], F32, name=f"encoding{c}_{h}") for h in range(PIECES)]
+            [held.tile([P, HALF], F32, name=f"encoding{c}_{half}") for half in range(2)]
             for c in range(FEATURE_BLOCKS)
         ]
-        for h in range(PIECES):
+        for half in range(2):
             for c in range(FEATURE_BLOCKS):
                 nc.scalar.dma_start(
-                    encoding[c][h][:], pe[c * P : (c + 1) * P, h * PIECE : (h + 1) * PIECE]
+                    encoding[c][half][:], pe[c * P : (c + 1) * P, half * HALF : (half + 1) * HALF]
                 )
         weights = [held.tile([P, WORDS], BF16, name=f"weights{c}") for c in range(FEATURE_BLOCKS)]
         for c in range(FEATURE_BLOCKS):
@@ -48,41 +49,45 @@ def tile_captioningtransformer_kernel(tc, emb, pe, w_vocab, b_vocab, offs, out):
             nc.sync.dma_start(bias[v][:], b_vocab[v * P : (v + 1) * P, :])
 
         def embed(h):
-            rounded = []
+            start, width = STARTS[h], WIDTHS[h]
+            moving = []
             for c in range(FEATURE_BLOCKS):
-                summed = held.tile([P, PIECE], F32, name=f"summed{c}_{h}")
-                picked = table[c][:].indirect(
-                    offsets[:, h * OFFSET_COLUMNS : (h + 1) * OFFSET_COLUMNS]
+                summed = held.tile([P, width], F32, name=f"summed{c}_{h}")
+                picked = table[c][:].indirect(offsets[:, start // 16 : (start + width) // 16])
+                nc.vector.tensor_tensor(
+                    summed[:],
+                    picked,
+                    encoding[c][start // HALF][:, start % HALF : start % HALF + width],
+                    ADD,
                 )
-                nc.vector.tensor_tensor(summed[:], picked, encoding[c][h][:], ADD)
-                moving = held.tile([P, PIECE], BF16, name=f"moving{c}_{h}")
-                nc.scalar.activation(moving[:], summed[:], COPY)
-                rounded.append(moving)
-            return rounded
+                rounded = held.tile([P, width], BF16, name=f"rounded{c}_{h}")
+                if h == len(WIDTHS) - 1 and c == FEATURE_BLOCKS - 1:
+                    nc.vector.tensor_copy(rounded[:], summed[:])
+                else:
+                    nc.scalar.activation(rounded[:], summed[:], COPY)
+                moving.append(rounded)
+            return moving
 
-        def project(h, rounded):
-            scores = [
-                banks.tile([P, PIECE], F32, name=f"scores{v}_{h}") for v in range(WORD_BLOCKS)
-            ]
+        def project(h, moving):
+            start, width = STARTS[h], WIDTHS[h]
+            scores = [banks.tile([P, width], F32, name=f"scores{v}_{h}") for v in range(WORD_BLOCKS)]
             for c in range(FEATURE_BLOCKS):
                 for v in range(WORD_BLOCKS):
                     nc.tensor.matmul(
                         scores[v][:],
                         weights[c][:, v * P : (v + 1) * P],
-                        rounded[c][:],
+                        moving[c][:],
                         start=(c == 0),
                         stop=(c == FEATURE_BLOCKS - 1),
                     )
             for v in range(WORD_BLOCKS):
-                staged = held.tile([P, PIECE], F32, name=f"staged{v}_{h}")
+                staged = held.tile([P, width], F32, name=f"staged{v}_{h}")
                 if v % 2 == 0:
                     nc.scalar.activation(staged[:], scores[v][:], IDENTITY, bias=bias[v][:])
                 else:
                     nc.vector.tensor_scalar_add(staged[:], scores[v][:], bias[v][:])
-                nc.sync.dma_start(
-                    out[v * P : (v + 1) * P, h * PIECE : (h + 1) * PIECE], staged[:]
-                )
+                nc.sync.dma_start(out[v * P : (v + 1) * P, start : start + width], staged[:])
 
-        rounded = [embed(h) for h in range(PIECES)]
-        for h in range(PIECES):
-            project(h, rounded[h])
+        embedded = [embed(h) for h in range(len(WIDTHS))]
+        for h in range(len(WIDTHS)):
+            project(h, embedded[h])

@@ -18,6 +18,8 @@ WIDTHS = (256, 256)
 assert sum(WIDTHS) == PLACES
 STARTS = [sum(WIDTHS[:h]) for h in range(len(WIDTHS))]
 
+WARM_MATMULS = 7
+
 FLOPS = 2 * FEATURES * WORDS * PLACES
 
 
@@ -48,6 +50,12 @@ def tile_captioningtransformer_kernel(tc, emb, pe, w_vocab, b_vocab, offs, out):
         for v in range(WORD_BLOCKS):
             nc.sync.dma_start(bias[v][:], b_vocab[v * P : (v + 1) * P, :])
 
+        zeros = held.tile([P, PLACES], BF16, name="zeros")
+        nc.vector.memset(zeros[:], 0.0)
+        unread = banks.tile([P, PLACES], F32, name="unread")
+        for repeat in range(WARM_MATMULS):
+            nc.tensor.matmul(unread[:], zeros[:, 0:P], zeros[:], start=True, stop=True)
+
         def embed(h):
             start, width = STARTS[h], WIDTHS[h]
             moving = []
@@ -61,10 +69,7 @@ def tile_captioningtransformer_kernel(tc, emb, pe, w_vocab, b_vocab, offs, out):
                     ADD,
                 )
                 rounded = held.tile([P, width], BF16, name=f"rounded{c}_{h}")
-                if h == len(WIDTHS) - 1 and c == FEATURE_BLOCKS - 1:
-                    nc.vector.tensor_copy(rounded[:], summed[:])
-                else:
-                    nc.scalar.activation(rounded[:], summed[:], COPY)
+                nc.scalar.activation(rounded[:], summed[:], COPY)
                 moving.append(rounded)
             return moving
 

@@ -69,7 +69,10 @@ def tile_captioningtransformer_kernel(tc, emb, pe, w_vocab, b_vocab, offs, out):
                     ADD,
                 )
                 rounded = held.tile([P, width], BF16, name=f"rounded{c}_{h}")
-                nc.scalar.activation(rounded[:], summed[:], COPY)
+                if h == len(WIDTHS) - 1 and c == FEATURE_BLOCKS - 1:
+                    nc.vector.tensor_copy(rounded[:], summed[:])
+                else:
+                    nc.scalar.activation(rounded[:], summed[:], COPY)
                 moving.append(rounded)
             return moving
 

@@ -43,12 +43,11 @@ def tile_captioningtransformer_kernel(tc, emb, pe, w_vocab, b_vocab, offs, out):
                 nc.scalar.dma_start(
                     encoding[c][half][:], pe[c * P : (c + 1) * P, half * HALF : (half + 1) * HALF]
                 )
-        weights = [held.tile([P, WORDS], BF16, name=f"weights{c}") for c in range(FEATURE_BLOCKS)]
-        for c in range(FEATURE_BLOCKS):
-            nc.gpsimd.dma_start(weights[c][:], w_vocab[c * P : (c + 1) * P, :])
+        weights = held.tile([P, FEATURE_BLOCKS, WORDS], BF16, name="weights")
+        nc.sync.dma_start(weights[:], w_vocab.rearrange("(c p) v -> p c v", p=P))
         bias = [held.tile([P, 1], F32, name=f"bias{v}") for v in range(WORD_BLOCKS)]
         for v in range(WORD_BLOCKS):
-            nc.sync.dma_start(bias[v][:], b_vocab[v * P : (v + 1) * P, :])
+            nc.gpsimd.dma_start(bias[v][:], b_vocab[v * P : (v + 1) * P, :])
 
         zeros = held.tile([P, PLACES], BF16, name="zeros")
         nc.vector.memset(zeros[:], 0.0)
@@ -83,7 +82,7 @@ def tile_captioningtransformer_kernel(tc, emb, pe, w_vocab, b_vocab, offs, out):
                 for v in range(WORD_BLOCKS):
                     nc.tensor.matmul(
                         scores[v][:],
-                        weights[c][:, v * P : (v + 1) * P],
+                        weights[:, c, v * P : (v + 1) * P],
                         moving[c][:],
                         start=(c == 0),
                         stop=(c == FEATURE_BLOCKS - 1),

@@ -14,7 +14,7 @@ PLACES = 512
 FEATURE_BLOCKS = FEATURES // P
 WORD_BLOCKS = WORDS // P
 HALF = PLACES // 2
-WIDTHS = (256, 256)
+WIDTHS = (256, 128, 128)
 assert sum(WIDTHS) == PLACES
 STARTS = [sum(WIDTHS[:h]) for h in range(len(WIDTHS))]
 

@@ -14,9 +14,9 @@ PLACES = 512
 FEATURE_BLOCKS = FEATURES // P
 WORD_BLOCKS = WORDS // P
 HALF = PLACES // 2
-WIDTHS = (256, 128, 128)
-assert sum(WIDTHS) == PLACES
-STARTS = [sum(WIDTHS[:h]) for h in range(len(WIDTHS))]
+PIECE = 128
+PIECES = PLACES // PIECE
+PIECES_IN_HALF = HALF // PIECE
 
 WARM_MATMULS = 7
 
@@ -30,71 +30,87 @@ def tile_captioningtransformer_kernel(tc, emb, pe, w_vocab, b_vocab, offs, out):
         tc.psum_pool(name="banks", bufs=1) as banks,
     ):
         offsets = held.tile([P, PLACES // 16], U16, name="offsets")
-        nc.sync.dma_start(offsets[:], offs)
         table = [held.tile([P, WORDS], F32, name=f"table{c}") for c in range(FEATURE_BLOCKS)]
-        for c in range(FEATURE_BLOCKS):
-            nc.sync.dma_start(table[c][:], emb[c * P : (c + 1) * P, :])
         encoding = [
             [held.tile([P, HALF], F32, name=f"encoding{c}_{half}") for half in range(2)]
             for c in range(FEATURE_BLOCKS)
         ]
-        for half in range(2):
-            for c in range(FEATURE_BLOCKS):
-                nc.scalar.dma_start(
-                    encoding[c][half][:], pe[c * P : (c + 1) * P, half * HALF : (half + 1) * HALF]
-                )
         weights = held.tile([P, FEATURE_BLOCKS, WORDS], BF16, name="weights")
-        nc.sync.dma_start(weights[:], w_vocab.rearrange("(c p) v -> p c v", p=P))
         bias = [held.tile([P, 1], F32, name=f"bias{v}") for v in range(WORD_BLOCKS)]
+
+        nc.sync.dma_start(offsets[:], offs)
+        for c in range(FEATURE_BLOCKS):
+            nc.sync.dma_start(table[c][:], emb[c * P : (c + 1) * P, :])
+            nc.scalar.dma_start(encoding[c][0][:], pe[c * P : (c + 1) * P, 0:HALF])
+        nc.sync.dma_start(weights[:], w_vocab.rearrange("(c p) v -> p c v", p=P))
+        for c in range(FEATURE_BLOCKS):
+            nc.sync.dma_start(encoding[c][1][:], pe[c * P : (c + 1) * P, HALF:PLACES])
         for v in range(WORD_BLOCKS):
             nc.gpsimd.dma_start(bias[v][:], b_vocab[v * P : (v + 1) * P, :])
 
         zeros = held.tile([P, PLACES], BF16, name="zeros")
         nc.vector.memset(zeros[:], 0.0)
-        unread = banks.tile([P, PLACES], F32, name="unread")
+        unread = banks.tile([P, PLACES], F32, name="unread", tag="last_bank")
         for repeat in range(WARM_MATMULS):
             nc.tensor.matmul(unread[:], zeros[:, 0:P], zeros[:], start=True, stop=True)
 
-        def embed(h):
-            start, width = STARTS[h], WIDTHS[h]
-            moving = []
-            for c in range(FEATURE_BLOCKS):
-                summed = held.tile([P, width], F32, name=f"summed{c}_{h}")
-                picked = table[c][:].indirect(offsets[:, start // 16 : (start + width) // 16])
-                nc.vector.tensor_tensor(
-                    summed[:],
-                    picked,
-                    encoding[c][start // HALF][:, start % HALF : start % HALF + width],
-                    ADD,
+        scores = [
+            [
+                banks.tile(
+                    [P, PIECE],
+                    F32,
+                    name=f"scores{v}_{h}",
+                    tag="last_bank" if (v, h) == (WORD_BLOCKS - 1, PIECES - 1) else f"scores{v}_{h}",
                 )
-                rounded = held.tile([P, width], BF16, name=f"rounded{c}_{h}")
-                if h == len(WIDTHS) - 1 and c == FEATURE_BLOCKS - 1:
+                for h in range(PIECES)
+            ]
+            for v in range(WORD_BLOCKS)
+        ]
+
+        def look_up(c, start, width):
+            summed = held.tile([P, width], F32, name=f"summed{c}_{start}")
+            picked = table[c][:].indirect(offsets[:, start // 16 : (start + width) // 16])
+            nc.vector.tensor_tensor(
+                summed[:], picked, encoding[c][start // HALF][:, start % HALF : start % HALF + width], ADD
+            )
+            return summed
+
+        def multiply(c, h, moving):
+            for v in range(WORD_BLOCKS):
+                nc.tensor.matmul(
+                    scores[v][h][:],
+                    weights[:, c, v * P : (v + 1) * P],
+                    moving,
+                    start=(c == 0),
+                    stop=(c == FEATURE_BLOCKS - 1),
+                )
+
+        def evacuate(h):
+            staged = held.tile([P, WORD_BLOCKS, PIECE], F32, name=f"staged{h}")
+            nc.scalar.activation(staged[:, 0, :], scores[0][h][:], IDENTITY, bias=bias[0][:])
+            nc.vector.tensor_scalar_add(staged[:, 1, :], scores[1][h][:], bias[1][:])
+            nc.sync.dma_start(
+                out.rearrange("(v p) j -> p v j", p=P)[:, :, h * PIECE : (h + 1) * PIECE], staged[:]
+            )
+
+        for half in range(2):
+            first = half * PIECES_IN_HALF
+            summed = look_up(0, half * HALF, HALF)
+            if half == 1:
+                evacuate(0)
+            rounded = held.tile([P, HALF], BF16, name=f"rounded0_{half}")
+            nc.scalar.activation(rounded[:], summed[:], COPY)
+            for h in range(first, first + PIECES_IN_HALF):
+                multiply(0, h, rounded[:, (h - first) * PIECE : (h - first + 1) * PIECE])
+            for h in range(first, first + PIECES_IN_HALF):
+                summed = look_up(1, h * PIECE, PIECE)
+                if h == first and half == 1:
+                    evacuate(1)
+                rounded = held.tile([P, PIECE], BF16, name=f"rounded1_{h}")
+                if h == PIECES - 1:
                     nc.vector.tensor_copy(rounded[:], summed[:])
                 else:
                     nc.scalar.activation(rounded[:], summed[:], COPY)
-                moving.append(rounded)
-            return moving
-
-        def project(h, moving):
-            start, width = STARTS[h], WIDTHS[h]
-            scores = [banks.tile([P, width], F32, name=f"scores{v}_{h}") for v in range(WORD_BLOCKS)]
-            for c in range(FEATURE_BLOCKS):
-                for v in range(WORD_BLOCKS):
-                    nc.tensor.matmul(
-                        scores[v][:],
-                        weights[:, c, v * P : (v + 1) * P],
-                        moving[c][:],
-                        start=(c == 0),
-                        stop=(c == FEATURE_BLOCKS - 1),
-                    )
-            for v in range(WORD_BLOCKS):
-                staged = held.tile([P, width], F32, name=f"staged{v}_{h}")
-                if v % 2 == 0:
-                    nc.scalar.activation(staged[:], scores[v][:], IDENTITY, bias=bias[v][:])
-                else:
-                    nc.vector.tensor_scalar_add(staged[:], scores[v][:], bias[v][:])
-                nc.sync.dma_start(out[v * P : (v + 1) * P, start : start + width], staged[:])
-
-        embedded = [embed(h) for h in range(len(WIDTHS))]
-        for h in range(len(WIDTHS)):
-            project(h, embedded[h])
+                multiply(1, h, rounded[:])
+        evacuate(2)
+        evacuate(3)

@@ -88,7 +88,10 @@ def tile_captioningtransformer_kernel(tc, emb, pe, w_vocab, b_vocab, offs, out):
         def evacuate(h):
             staged = held.tile([P, WORD_BLOCKS, PIECE], F32, name=f"staged{h}")
             nc.scalar.activation(staged[:, 0, :], scores[0][h][:], IDENTITY, bias=bias[0][:])
-            nc.vector.tensor_scalar_add(staged[:, 1, :], scores[1][h][:], bias[1][:])
+            if h < PIECES_IN_HALF:
+                nc.scalar.activation(staged[:, 1, :], scores[1][h][:], IDENTITY, bias=bias[1][:])
+            else:
+                nc.vector.tensor_scalar_add(staged[:, 1, :], scores[1][h][:], bias[1][:])
             nc.sync.dma_start(
                 out.rearrange("(v p) j -> p v j", p=P)[:, :, h * PIECE : (h + 1) * PIECE], staged[:]
             )
@@ -104,13 +107,13 @@ def tile_captioningtransformer_kernel(tc, emb, pe, w_vocab, b_vocab, offs, out):
                 multiply(0, h, rounded[:, (h - first) * PIECE : (h - first + 1) * PIECE])
             for h in range(first, first + PIECES_IN_HALF):
                 summed = look_up(1, h * PIECE, PIECE)
-                if h == first and half == 1:
-                    evacuate(1)
                 rounded = held.tile([P, PIECE], BF16, name=f"rounded1_{h}")
                 if h == PIECES - 1:
                     nc.vector.tensor_copy(rounded[:], summed[:])
                 else:
                     nc.scalar.activation(rounded[:], summed[:], COPY)
                 multiply(1, h, rounded[:])
+                if h == first and half == 1:
+                    evacuate(1)
         evacuate(2)
         evacuate(3)

@@ -13,10 +13,9 @@ WORDS = 256
 PLACES = 512
 FEATURE_BLOCKS = FEATURES // P
 WORD_BLOCKS = WORDS // P
-HALF = PLACES // 2
 PIECE = 128
 PIECES = PLACES // PIECE
-PIECES_IN_HALF = HALF // PIECE
+LOOK_UPS = ((0, 0, 2), (0, 2, 1), (1, 0, 1), (1, 1, 1), (0, 3, 1), (1, 2, 1), (1, 3, 1))
 
 WARM_MATMULS = 7
 
@@ -32,19 +31,27 @@ def tile_captioningtransformer_kernel(tc, emb, pe, w_vocab, b_vocab, offs, out):
         offsets = held.tile([P, PLACES // 16], U16, name="offsets")
         table = [held.tile([P, WORDS], F32, name=f"table{c}") for c in range(FEATURE_BLOCKS)]
         encoding = [
-            [held.tile([P, HALF], F32, name=f"encoding{c}_{half}") for half in range(2)]
-            for c in range(FEATURE_BLOCKS)
+            held.tile([P, pieces * PIECE], F32, name=f"encoding{c}_{first}") for c, first, pieces in LOOK_UPS
         ]
         weights = held.tile([P, FEATURE_BLOCKS, WORDS], BF16, name="weights")
         bias = [held.tile([P, 1], F32, name=f"bias{v}") for v in range(WORD_BLOCKS)]
 
+        def load_encoding(queue, step):
+            c, first, pieces = LOOK_UPS[step]
+            queue.dma_start(
+                encoding[step][:], pe[c * P : (c + 1) * P, first * PIECE : (first + pieces) * PIECE]
+            )
+
         nc.sync.dma_start(offsets[:], offs)
-        for c in range(FEATURE_BLOCKS):
-            nc.sync.dma_start(table[c][:], emb[c * P : (c + 1) * P, :])
-            nc.scalar.dma_start(encoding[c][0][:], pe[c * P : (c + 1) * P, 0:HALF])
+        nc.sync.dma_start(table[0][:], emb[0:P, :])
+        load_encoding(nc.scalar, 0)
+        load_encoding(nc.sync, 1)
+        nc.sync.dma_start(table[1][:], emb[P : 2 * P, :])
+        load_encoding(nc.scalar, 2)
+        load_encoding(nc.scalar, 3)
         nc.sync.dma_start(weights[:], w_vocab.rearrange("(c p) v -> p c v", p=P))
-        for c in range(FEATURE_BLOCKS):
-            nc.sync.dma_start(encoding[c][1][:], pe[c * P : (c + 1) * P, HALF:PLACES])
+        for step in range(4, len(LOOK_UPS)):
+            load_encoding(nc.sync, step)
         for v in range(WORD_BLOCKS):
             nc.gpsimd.dma_start(bias[v][:], b_vocab[v * P : (v + 1) * P, :])
 
@@ -67,14 +74,6 @@ def tile_captioningtransformer_kernel(tc, emb, pe, w_vocab, b_vocab, offs, out):
             for v in range(WORD_BLOCKS)
         ]
 
-        def look_up(c, start, width):
-            summed = held.tile([P, width], F32, name=f"summed{c}_{start}")
-            picked = table[c][:].indirect(offsets[:, start // 16 : (start + width) // 16])
-            nc.vector.tensor_tensor(
-                summed[:], picked, encoding[c][start // HALF][:, start % HALF : start % HALF + width], ADD
-            )
-            return summed
-
         def multiply(c, h, moving):
             for v in range(WORD_BLOCKS):
                 nc.tensor.matmul(
@@ -88,7 +87,7 @@ def tile_captioningtransformer_kernel(tc, emb, pe, w_vocab, b_vocab, offs, out):
         def evacuate(h):
             staged = held.tile([P, WORD_BLOCKS, PIECE], F32, name=f"staged{h}")
             nc.scalar.activation(staged[:, 0, :], scores[0][h][:], IDENTITY, bias=bias[0][:])
-            if h < PIECES_IN_HALF:
+            if h < PIECES // 2:
                 nc.scalar.activation(staged[:, 1, :], scores[1][h][:], IDENTITY, bias=bias[1][:])
             else:
                 nc.vector.tensor_scalar_add(staged[:, 1, :], scores[1][h][:], bias[1][:])
@@ -96,24 +95,21 @@ def tile_captioningtransformer_kernel(tc, emb, pe, w_vocab, b_vocab, offs, out):
                 out.rearrange("(v p) j -> p v j", p=P)[:, :, h * PIECE : (h + 1) * PIECE], staged[:]
             )
 
-        for half in range(2):
-            first = half * PIECES_IN_HALF
-            summed = look_up(0, half * HALF, HALF)
-            if half == 1:
+        for step, (c, first, pieces) in enumerate(LOOK_UPS):
+            width = pieces * PIECE
+            summed = held.tile([P, width], F32, name=f"summed{step}")
+            picked = table[c][:].indirect(offsets[:, first * PIECE // 16 : (first + pieces) * PIECE // 16])
+            nc.vector.tensor_tensor(summed[:], picked, encoding[step][:], ADD)
+            if step == len(LOOK_UPS) - 3:
                 evacuate(0)
-            rounded = held.tile([P, HALF], BF16, name=f"rounded0_{half}")
-            nc.scalar.activation(rounded[:], summed[:], COPY)
-            for h in range(first, first + PIECES_IN_HALF):
-                multiply(0, h, rounded[:, (h - first) * PIECE : (h - first + 1) * PIECE])
-            for h in range(first, first + PIECES_IN_HALF):
-                summed = look_up(1, h * PIECE, PIECE)
-                rounded = held.tile([P, PIECE], BF16, name=f"rounded1_{h}")
-                if h == PIECES - 1:
-                    nc.vector.tensor_copy(rounded[:], summed[:])
-                else:
-                    nc.scalar.activation(rounded[:], summed[:], COPY)
-                multiply(1, h, rounded[:])
-                if h == first and half == 1:
-                    evacuate(1)
+            rounded = held.tile([P, width], BF16, name=f"rounded{step}")
+            if step == len(LOOK_UPS) - 1:
+                nc.vector.tensor_copy(rounded[:], summed[:])
+            else:
+                nc.scalar.activation(rounded[:], summed[:], COPY)
+            for k in range(pieces):
+                multiply(c, first + k, rounded[:, k * PIECE : (k + 1) * PIECE])
+            if step == len(LOOK_UPS) - 2:
+                evacuate(1)
         evacuate(2)
         evacuate(3)

import concourse.mybir as mybir

F32 = mybir.dt.float32
BF16 = mybir.dt.bfloat16
U16 = mybir.dt.uint16
ADD = mybir.AluOpType.add
COPY = mybir.ActivationFunctionType.Copy
IDENTITY = mybir.ActivationFunctionType.Identity

P = 128
FEATURES = 256
WORDS = 256
PLACES = 512
FEATURE_BLOCKS = FEATURES // P
WORD_BLOCKS = WORDS // P
PIECE = 128
PIECES = PLACES // PIECE
LOOK_UPS = ((0, 0, 2), (0, 2, 1), (1, 0, 1), (1, 1, 1), (0, 3, 1), (1, 2, 1), (1, 3, 1))

WARM_MATMULS = 7

FLOPS = 2 * FEATURES * WORDS * PLACES


def tile_captioningtransformer_kernel(tc, emb, pe, w_vocab, b_vocab, offs, out):
    nc = tc.nc
    with (
        tc.tile_pool(name="held", bufs=1) as held,
        tc.psum_pool(name="banks", bufs=1) as banks,
    ):
        offsets = held.tile([P, PLACES // 16], U16, name="offsets")
        table = [held.tile([P, WORDS], F32, name=f"table{c}") for c in range(FEATURE_BLOCKS)]
        encoding = [
            held.tile([P, pieces * PIECE], F32, name=f"encoding{c}_{first}") for c, first, pieces in LOOK_UPS
        ]
        weights = held.tile([P, FEATURE_BLOCKS, WORDS], BF16, name="weights")
        bias = [held.tile([P, 1], F32, name=f"bias{v}") for v in range(WORD_BLOCKS)]

        def load_encoding(queue, step):
            c, first, pieces = LOOK_UPS[step]
            queue.dma_start(
                encoding[step][:], pe[c * P : (c + 1) * P, first * PIECE : (first + pieces) * PIECE]
            )

        nc.sync.dma_start(offsets[:], offs)
        nc.sync.dma_start(table[0][:], emb[0:P, :])
        load_encoding(nc.scalar, 0)
        load_encoding(nc.sync, 1)
        nc.sync.dma_start(table[1][:], emb[P : 2 * P, :])
        load_encoding(nc.scalar, 2)
        load_encoding(nc.scalar, 3)
        nc.sync.dma_start(weights[:], w_vocab.rearrange("(c p) v -> p c v", p=P))
        for step in range(4, len(LOOK_UPS)):
            load_encoding(nc.sync, step)
        for v in range(WORD_BLOCKS):
            nc.gpsimd.dma_start(bias[v][:], b_vocab[v * P : (v + 1) * P, :])

        zeros = held.tile([P, PLACES], BF16, name="zeros")
        nc.vector.memset(zeros[:], 0.0)
        unread = banks.tile([P, PLACES], F32, name="unread", tag="last_bank")
        for repeat in range(WARM_MATMULS):
            nc.tensor.matmul(unread[:], zeros[:, 0:P], zeros[:], start=True, stop=True)

        scores = [
            [
                banks.tile(
                    [P, PIECE],
                    F32,
                    name=f"scores{v}_{h}",
                    tag="last_bank" if (v, h) == (WORD_BLOCKS - 1, PIECES - 1) else f"scores{v}_{h}",
                )
                for h in range(PIECES)
            ]
            for v in range(WORD_BLOCKS)
        ]

        def multiply(c, h, moving):
            for v in range(WORD_BLOCKS):
                nc.tensor.matmul(
                    scores[v][h][:],
                    weights[:, c, v * P : (v + 1) * P],
                    moving,
                    start=(c == 0),
                    stop=(c == FEATURE_BLOCKS - 1),
                )

        def evacuate(h):
            staged = held.tile([P, WORD_BLOCKS, PIECE], F32, name=f"staged{h}")
            nc.scalar.activation(staged[:, 0, :], scores[0][h][:], IDENTITY, bias=bias[0][:])
            if h < PIECES // 2:
                nc.scalar.activation(staged[:, 1, :], scores[1][h][:], IDENTITY, bias=bias[1][:])
            else:
                nc.vector.tensor_scalar_add(staged[:, 1, :], scores[1][h][:], bias[1][:])
            nc.sync.dma_start(
                out.rearrange("(v p) j -> p v j", p=P)[:, :, h * PIECE : (h + 1) * PIECE], staged[:]
            )

        for step, (c, first, pieces) in enumerate(LOOK_UPS):
            width = pieces * PIECE
            summed = held.tile([P, width], F32, name=f"summed{step}")
            picked = table[c][:].indirect(offsets[:, first * PIECE // 16 : (first + pieces) * PIECE // 16])
            nc.vector.tensor_tensor(summed[:], picked, encoding[step][:], ADD)
            if step == len(LOOK_UPS) - 3:
                evacuate(0)
            rounded = held.tile([P, width], BF16, name=f"rounded{step}")
            if step == len(LOOK_UPS) - 1:
                nc.vector.tensor_copy(rounded[:], summed[:])
            else:
                nc.scalar.activation(rounded[:], summed[:], COPY)
            for k in range(pieces):
                multiply(c, first + k, rounded[:, k * PIECE : (k + 1) * PIECE])
            if step == len(LOOK_UPS) - 2:
                evacuate(1)
        evacuate(2)
        evacuate(3)
